import numpy as np
import ml_dtypes


def mxq(x, axis, fmt="e4m3"):
    dtype, down = {"e4m3": (ml_dtypes.float8_e4m3fn, 7), "e5m2": (ml_dtypes.float8_e5m2, 14)}[fmt]
    v = np.moveaxis(np.asarray(x, np.float32).astype(ml_dtypes.bfloat16).astype(np.float64), axis, -1)
    blocks = v.reshape(v.shape[:-1] + (-1, 32))
    amax = np.abs(blocks).max(-1, keepdims=True)
    byte = np.maximum(np.where(amax > 0, np.frexp(amax)[1] - 1 + 127, 0) - down, 1)
    scale = np.exp2(byte - 127.0)
    codes = (blocks / scale).astype(np.float32).astype(dtype).astype(np.float64)
    return np.moveaxis((codes * scale).reshape(v.shape), -1, axis)


WIDE = False


def mx_kscale(k):
    if not WIDE:
        return np.ones(k)
    levels = np.array([10, -10, 5, -5, 0])
    a = np.random.permutation(np.resize(levels, k // 512 * 4)).reshape(k // 512, 4)
    idx = np.arange(k)
    return np.exp2(a[idx // 512, idx % 128 // 32])


BF16 = ml_dtypes.bfloat16


def bf(x):
    return np.asarray(x, np.float32).astype(BF16)


def f64(x):
    return np.asarray(x).astype(np.float64)


NB, S, D, O, E, R = 4, 1024, 1024, 256, 32, 16
ER = E * R
SCALING = 2.0


def softmax(v):
    e = np.exp(v - v.max(-1, keepdims=True))
    return e / e.sum(-1, keepdims=True)


def setup_inputs():
    s, t = mx_kscale(D), mx_kscale(ER)
    return {
        "x": bf(np.random.standard_normal((NB, S, D)) * s),
        "gate_logits": bf(np.random.standard_normal((NB, S, E)) * 1.5),
        "W_base": bf(np.random.standard_normal((O, D)) / np.sqrt(D) / s),
        "b_base": bf(np.random.standard_normal(O) * 0.3),
        "A": bf(np.random.standard_normal((E, R, D)) / np.sqrt(D) / s * t.reshape(E, R, 1)),
        "B": bf(np.random.standard_normal((E, O, R)) / np.sqrt(R) / t.reshape(E, 1, R)),
    }


def reference(x, gate_logits, W_base, b_base, A, B):
    xq = mxq(f64(x), 2, "e4m3")
    result = (xq @ mxq(f64(W_base), 1, "e4m3").T) + f64(b_base)
    route = softmax(f64(gate_logits))
    h = (xq @ mxq(f64(A).reshape(ER, D), 1, "e4m3").T).reshape(NB, S, E, R)
    hw = (h * route[..., None]).reshape(NB, S, ER)
    b_flat = f64(B).transpose(0, 2, 1).reshape(ER, O)
    return result + SCALING * (mxq(hw, 2, "e4m3") @ mxq(b_flat, 0, "e4m3"))

@@ -1,0 +1,352 @@
+from contextlib import ExitStack
+
+import concourse.masks as masks
+import concourse.mybir as mybir
+
+F32 = mybir.dt.float32
+BF16 = mybir.dt.bfloat16
+U32 = mybir.dt.uint32
+U8 = mybir.dt.uint8
+FP8X4 = mybir.dt.float8_e4m3fn_x4
+ALU = mybir.AluOpType
+ACT = mybir.ActivationFunctionType
+AXIS = mybir.AxisListType
+
+P = 128
+PACK = 4
+TOKENS = 4096
+D = 1024
+O = 256
+E = 32
+RANK = 16
+ER = E * RANK
+SCALING = 2.0
+PASSES = D // (P * PACK)
+WORDS = D // 2
+BANK = 512
+SLOTS = TOKENS // P
+ROUND = 4
+ROUNDS = SLOTS // ROUND
+O_TILES = O // P
+LAG = 3
+
+FLOPS = 2 * TOKENS * D * (O + ER) + 2 * TOKENS * ER * O
+
+
+def tile_linearmoloralayer_pa_t_kernel(tc, x, gate_logits, W_base, b_base, A, B, out):
+    nc = tc.nc
+
+    x_view = x.flatten_outer_dims().rearrange("(p s) d -> p s d", s=SLOTS)
+    gate_view = gate_logits.flatten_outer_dims().rearrange("(p s) e -> p (s e)", s=SLOTS)
+    out_view = out.flatten_outer_dims().rearrange("(p s) o -> p s o", s=SLOTS)
+    a_view = A.flatten_outer_dims().rearrange("(q c) d -> q c d", c=PACK)
+    w_view = W_base.rearrange("(h m) d -> m h d", m=P)
+    b_view = B.rearrange("e (m h) r -> m e (h r)", h=O_TILES)
+
+    with ExitStack() as ctx:
+        keep = ctx.enter_context(tc.tile_pool(name="keep", bufs=1))
+        xg_pool = ctx.enter_context(tc.tile_pool(name="xg_pool", bufs=2))
+        xq_pool = ctx.enter_context(tc.tile_pool(name="xq_pool", bufs=LAG + 2))
+        route_pool = ctx.enter_context(tc.tile_pool(name="route_pool", bufs=2))
+        hwg_pool = ctx.enter_context(tc.tile_pool(name="hwg_pool", bufs=2))
+        hwq_pool = ctx.enter_context(tc.tile_pool(name="hwq_pool", bufs=LAG + 1))
+        stage_pool = ctx.enter_context(tc.tile_pool(name="stage_pool", bufs=3))
+        t_psum = ctx.enter_context(tc.psum_pool(name="t_psum", bufs=4))
+        h_psum = ctx.enter_context(tc.psum_pool(name="h_psum", bufs=2))
+        o_psum = ctx.enter_context(tc.psum_pool(name="o_psum", bufs=2))
+        ctx.enter_context(tc.manual_schedule())
+
+        ident = keep.tile([P, P], F32)
+        masks.make_identity(nc, ident[:])
+
+        gate_sb = keep.tile([P, SLOTS * E], BF16)
+        a_raw = [keep.tile([P, D], BF16, name="a_raw%d" % c) for c in range(PACK)]
+        x_raw = [keep.tile([P, D], BF16, name="x_raw%d" % s) for s in range(SLOTS)]
+        w_raw = keep.tile([P, O_TILES * D], BF16)
+        b_raw = keep.tile([P, O_TILES * ER], BF16)
+        bias_sb = keep.tile([P, O], BF16)
+
+        def load_x(first, last):
+            for s in range(first, last):
+                nc.sync.dma_start(out=x_raw[s][:], in_=x_view[:, s, :])
+
+        nc.sync.dma_start(out=gate_sb[:], in_=gate_view)
+        for c in range(PACK):
+            nc.sync.dma_start(out=a_raw[c][:], in_=a_view[:, c, :])
+        load_x(0, 2 * ROUND)
+        nc.sync.dma_start(out=w_raw[:].rearrange("m (h d) -> m h d", h=O_TILES), in_=w_view)
+        load_x(2 * ROUND, 3 * ROUND)
+        nc.sync.dma_start(out=b_raw[:].rearrange("m (e f) -> m e f", e=E), in_=b_view)
+        nc.sync.dma_start(out=bias_sb[:], in_=b_base.partition_broadcast(P))
+        load_x(3 * ROUND, SLOTS)
+
+        def transpose_rows(bank, words):
+            for block in range(WORDS // P):
+                cols = slice(block * P, (block + 1) * P)
+                nc.tensor.transpose(out=bank[:, cols], in_=words[:, cols], identity=ident[:])
+
+        def words_side_by_side(bank):
+            return bank[:].rearrange("q (g u m) -> q g m u", g=PASSES, u=2)
+
+        g_max = keep.tile([P, SLOTS], F32)
+        g_exp = keep.tile([P, SLOTS * E], F32)
+        g_sum = keep.tile([P, SLOTS], F32)
+        g_inv = keep.tile([P, SLOTS], F32)
+        route_wide = {}
+        route_t = {}
+
+        def by_slot(ap):
+            return ap.rearrange("p (s e) -> p s e", e=E)
+
+        def softmax_shift(first, last):
+            cols = slice(first * E, last * E)
+            nc.vector.tensor_reduce(
+                out=g_max[:, first:last], in_=by_slot(gate_sb[:, cols]), axis=AXIS.X, op=ALU.max
+            )
+            nc.vector.tensor_tensor(
+                out=by_slot(g_exp[:, cols]),
+                in0=by_slot(gate_sb[:, cols]),
+                in1=g_max[:, first:last].unsqueeze(2).to_broadcast([P, last - first, E]),
+                op=ALU.subtract,
+            )
+
+        def softmax_exp_norm(first, last):
+            cols = slice(first * E, last * E)
+            nc.scalar.activation(out=g_exp[:, cols], in_=g_exp[:, cols], func=ACT.Exp)
+            nc.vector.tensor_reduce(
+                out=g_sum[:, first:last], in_=by_slot(g_exp[:, cols]), axis=AXIS.X, op=ALU.add
+            )
+            nc.vector.reciprocal(out=g_inv[:, first:last], in_=g_sum[:, first:last])
+
+        def expand_route(r):
+            first = r * ROUND
+            wide = route_pool.tile([P, ROUND * P], F32, name="route_wide", tag="route_wide")
+            route_wide[r] = wide
+            shape = [P, ROUND, E, PACK]
+            nc.gpsimd.tensor_tensor(
+                out=wide[:].rearrange("p (s e i) -> p s e i", s=ROUND, i=PACK),
+                in0=by_slot(g_exp[:, first * E : (first + ROUND) * E]).unsqueeze(3).to_broadcast(shape),
+                in1=g_inv[:, first : first + ROUND].unsqueeze(2).unsqueeze(3).to_broadcast(shape),
+                op=ALU.mult,
+            )
+
+        def transpose_route(r):
+            bank = t_psum.tile([P, BANK], F32, name="route_bank", tag="t")
+            for j in range(ROUND):
+                cols = slice(j * P, (j + 1) * P)
+                nc.tensor.transpose(out=bank[:, cols], in_=route_wide[r][:, cols], identity=ident[:])
+            route_t[r] = route_pool.tile([P, ROUND * P], F32, name="route_t", tag="route_t")
+            nc.scalar.mul(out=route_t[r][:], in_=bank[:], mul=SCALING)
+
+        a_grouped = keep.tile([P, PACK * D], BF16, align_bytes=64)
+        a_codes = keep.tile([P, PACK * PASSES * P], U32, align_bytes=64)
+        a_scales = keep.tile([P, PACK * PASSES * P], U8, align_bytes=64)
+        w_grouped = keep.tile([P, O_TILES * D], BF16, align_bytes=64)
+        w_codes = keep.tile([P, PASSES * O], U32, align_bytes=64)
+        w_scales = keep.tile([P, PASSES * O], U8, align_bytes=64)
+        b_sorted = keep.tile([P, O_TILES * ER], BF16)
+        b_grouped = keep.tile([P, O * PACK], BF16, align_bytes=64)
+        b_codes = keep.tile([P, O], U32, align_bytes=64)
+        b_scales = keep.tile([P, O], U8, align_bytes=64)
+
+        def prepare_a_chunk(c):
+            bank = t_psum.tile([P, BANK], F32, name="a_bank", tag="t")
+            transpose_rows(bank, a_raw[c][:].bitcast(F32))
+            grouped_words = a_grouped[:].bitcast(F32).rearrange(
+                "q (c g m u) -> q c g m u", c=PACK, g=PASSES, u=2
+            )
+            nc.scalar.copy(out=grouped_words[:, c], in_=words_side_by_side(bank))
+            cols = slice(c * PASSES * P, (c + 1) * PASSES * P)
+            nc.vector.quantize_mx(
+                out=a_codes[:, cols].bitcast(FP8X4),
+                scales=a_scales[:, cols],
+                in_=a_grouped[:, c * D : (c + 1) * D],
+            )
+
+        def transpose_w():
+            grouped_words = w_grouped[:].bitcast(F32).rearrange(
+                "q (g h m u) -> q g h m u", g=PASSES, h=O_TILES, u=2
+            )
+            for h in range(O_TILES):
+                bank = t_psum.tile([P, BANK], F32, name="w_bank", tag="t")
+                transpose_rows(bank, w_raw[:].bitcast(F32)[:, h * WORDS : (h + 1) * WORDS])
+                nc.scalar.copy(out=grouped_words[:, :, h], in_=words_side_by_side(bank))
+
+        def quantise_w():
+            nc.vector.quantize_mx(
+                out=w_codes[:].bitcast(FP8X4), scales=w_scales[:], in_=w_grouped[:]
+            )
+
+        def sort_b():
+            nc.gpsimd.tensor_copy(
+                out=b_sorted[:].rearrange("m (h e r) -> m h e r", h=O_TILES, r=RANK),
+                in_=b_raw[:].rearrange("m (e h r) -> m h e r", h=O_TILES, r=RANK),
+            )
+
+        def transpose_b():
+            words = b_sorted[:].bitcast(F32).rearrange("m (h q u) -> m h u q", h=O_TILES, u=2)
+            bank = t_psum.tile([P, BANK], F32, name="b_bank", tag="t")
+            for h in range(O_TILES):
+                for u in range(2):
+                    cols = slice((h * 2 + u) * P, (h * 2 + u + 1) * P)
+                    nc.tensor.transpose(out=bank[:, cols], in_=words[:, h, u, :], identity=ident[:])
+            nc.scalar.copy(
+                out=b_grouped[:].bitcast(F32).rearrange("q (m h u) -> q m h u", h=O_TILES, u=2),
+                in_=bank[:].rearrange("q (h u m) -> q m h u", h=O_TILES, u=2),
+            )
+
+        def quantise_b():
+            nc.vector.quantize_mx(
+                out=b_codes[:].bitcast(FP8X4), scales=b_scales[:], in_=b_grouped[:]
+            )
+
+        x_grouped = {}
+        x_codes = {}
+        x_scales = {}
+
+        def transpose_x(r):
+            x_grouped[r] = xg_pool.tile([P, ROUND * D], BF16, name="x_grouped", tag="xg", align_bytes=64)
+            grouped_words = x_grouped[r][:].bitcast(F32).rearrange(
+                "q (j g w u) -> q j g w u", j=ROUND, g=PASSES, u=2
+            )
+            for j in range(ROUND):
+                bank = t_psum.tile([P, BANK], F32, name="x_bank", tag="t")
+                transpose_rows(bank, x_raw[r * ROUND + j][:].bitcast(F32))
+                nc.scalar.copy(out=grouped_words[:, j], in_=words_side_by_side(bank))
+
+        def quantise_x(r, j):
+            if j == 0:
+                width = ROUND * PASSES * P
+                x_codes[r] = xq_pool.tile([P, width], U32, name="x_codes", tag="xc", align_bytes=64)
+                x_scales[r] = xq_pool.tile([P, width], U8, name="x_scales", tag="xs", align_bytes=64)
+            cols = slice(j * PASSES * P, (j + 1) * PASSES * P)
+            nc.vector.quantize_mx(
+                out=x_codes[r][:, cols].bitcast(FP8X4),
+                scales=x_scales[r][:, cols],
+                in_=x_grouped[r][:, j * D : (j + 1) * D],
+            )
+
+        hw_grouped = {}
+        hw_codes = {}
+        hw_scales = {}
+        o_banks = {}
+        o_stage = {}
+
+        def project(r, j):
+            h_bank = h_psum.tile([P, BANK], F32, name="h_bank", tag="h")
+            for c in range(PACK):
+                for g in range(PASSES):
+                    a_cols = slice((c * PASSES + g) * P, (c * PASSES + g + 1) * P)
+                    x_cols = slice((j * PASSES + g) * P, (j * PASSES + g + 1) * P)
+                    nc.tensor.matmul_mx(
+                        out=h_bank[:, c * P : (c + 1) * P],
+                        lhsT=a_codes[:, a_cols].bitcast(FP8X4),
+                        lhsT_scale=a_scales[:, a_cols],
+                        rhs=x_codes[r][:, x_cols].bitcast(FP8X4),
+                        rhs_scale=x_scales[r][:, x_cols],
+                        start=(g == 0),
+                        stop=(g == PASSES - 1),
+                    )
+            if j == 0:
+                hw_grouped[r] = hwg_pool.tile(
+                    [P, ROUND * ER], BF16, name="hw_grouped", tag="hwg", align_bytes=64
+                )
+            nc.vector.tensor_tensor(
+                out=hw_grouped[r][:, j * ER : (j + 1) * ER].rearrange("q (w c) -> q w c", c=PACK),
+                in0=h_bank[:].rearrange("q (c w) -> q w c", c=PACK),
+                in1=route_t[r][:, j * P : (j + 1) * P].unsqueeze(2).to_broadcast([P, P, PACK]),
+                op=ALU.mult,
+            )
+
+        def quantise_hw(r):
+            hw_codes[r] = hwq_pool.tile([P, ROUND * P], U32, name="hw_codes", tag="hc", align_bytes=64)
+            hw_scales[r] = hwq_pool.tile([P, ROUND * P], U8, name="hw_scales", tag="hs", align_bytes=64)
+            nc.vector.quantize_mx(
+                out=hw_codes[r][:].bitcast(FP8X4), scales=hw_scales[r][:], in_=hw_grouped[r][:]
+            )
+
+        def emit_output(r, j):
+            half = j % 2
+            if half == 0:
+                o_banks[r] = o_psum.tile([P, BANK], F32, name="o_bank", tag="o")
+            o_cols = slice(half * O, (half + 1) * O)
+            for g in range(PASSES):
+                x_cols = slice((j * PASSES + g) * P, (j * PASSES + g + 1) * P)
+                nc.tensor.matmul_mx(
+                    out=o_banks[r][:, o_cols],
+                    lhsT=x_codes[r][:, x_cols].bitcast(FP8X4),
+                    lhsT_scale=x_scales[r][:, x_cols],
+                    rhs=w_codes[:, g * O : (g + 1) * O].bitcast(FP8X4),
+                    rhs_scale=w_scales[:, g * O : (g + 1) * O],
+                    start=(g == 0),
+                    stop=False,
+                )
+            nc.tensor.matmul_mx(
+                out=o_banks[r][:, o_cols],
+                lhsT=hw_codes[r][:, j * P : (j + 1) * P].bitcast(FP8X4),
+                lhsT_scale=hw_scales[r][:, j * P : (j + 1) * P],
+                rhs=b_codes[:].bitcast(FP8X4),
+                rhs_scale=b_scales[:],
+                start=False,
+                stop=True,
+            )
+            if j == 0:
+                o_stage[r] = stage_pool.tile([P, ROUND * O], F32, name="o_stage", tag="os")
+            if half == 1:
+                nc.vector.tensor_tensor(
+                    out=o_stage[r][:, (j - 1) * O : (j + 1) * O].rearrange("p (s o) -> p s o", o=O),
+                    in0=o_banks[r][:].rearrange("p (s o) -> p s o", o=O),
+                    in1=bias_sb[:].unsqueeze(1).to_broadcast([P, 2, O]),
+                    op=ALU.add,
+                )
+
+        def store(r):
+            nc.sync.dma_start(
+                out=out_view[:, r * ROUND : (r + 1) * ROUND, :],
+                in_=o_stage[r][:].rearrange("p (s o) -> p s o", o=O),
+            )
+
+        warm = keep.tile([P, 1], F32)
+        nc.vector.memset(warm[:], 0.0)
+        nc.scalar.activation(out=warm[:], in_=warm[:], func=ACT.Exp)
+
+        softmax_shift(0, ROUND)
+        softmax_exp_norm(0, ROUND)
+        softmax_shift(ROUND, SLOTS)
+        expand_route(0)
+        for c in range(PACK):
+            prepare_a_chunk(c)
+        softmax_exp_norm(ROUND, SLOTS)
+        expand_route(1)
+        transpose_route(0)
+        transpose_x(0)
+        for j in range(ROUND):
+            quantise_x(0, j)
+
+        for r in range(ROUNDS + LAG):
+            for j in range(ROUND):
+                if j == ROUND // 2 and r + 1 < ROUNDS:
+                    transpose_route(r + 1)
+                    transpose_x(r + 1)
+                    if r + 2 < ROUNDS:
+                        expand_route(r + 2)
+                    if r + 2 == LAG:
+                        transpose_w()
+                        sort_b()
+                    if r + 1 == LAG:
+                        transpose_b()
+                if r < ROUNDS:
+                    project(r, j)
+                if r >= LAG:
+                    emit_output(r - LAG, j)
+                if j >= ROUND // 2 and r + 1 < ROUNDS:
+                    quantise_x(r + 1, 2 * (j - ROUND // 2))
+                    quantise_x(r + 1, 2 * (j - ROUND // 2) + 1)
+            if r < ROUNDS:
+                quantise_hw(r)
+            if r + 2 == LAG:
+                quantise_w()
+            if r + 1 == LAG:
+                quantise_b()
+            if r >= LAG:
+                store(r - LAG)

@@ -25,10 +25,10 @@ PASSES = D // (P * PACK)
 WORDS = D // 2
 BANK = 512
 SLOTS = TOKENS // P
-ROUND = 4
-ROUNDS = SLOTS // ROUND
+UNIT = 2
+UNITS = SLOTS // UNIT
 O_TILES = O // P
-LAG = 3
+LAG = 4
 
 FLOPS = 2 * TOKENS * D * (O + ER) + 2 * TOKENS * ER * O
 
@@ -41,7 +41,7 @@ def tile_linearmoloralayer_pa_t_kernel(tc, x, gate_logits, W_base, b_base, A, B,
     out_view = out.flatten_outer_dims().rearrange("(p s) o -> p s o", s=SLOTS)
     a_view = A.flatten_outer_dims().rearrange("(q c) d -> q c d", c=PACK)
     w_view = W_base.rearrange("(h m) d -> m h d", m=P)
-    b_view = B.rearrange("e (m h) r -> m e (h r)", h=O_TILES)
+    b_view = B.rearrange("e (h m) r -> h m e r", m=P)
 
     with ExitStack() as ctx:
         keep = ctx.enter_context(tc.tile_pool(name="keep", bufs=1))
@@ -50,7 +50,7 @@ def tile_linearmoloralayer_pa_t_kernel(tc, x, gate_logits, W_base, b_base, A, B,
         route_pool = ctx.enter_context(tc.tile_pool(name="route_pool", bufs=2))
         hwg_pool = ctx.enter_context(tc.tile_pool(name="hwg_pool", bufs=2))
         hwq_pool = ctx.enter_context(tc.tile_pool(name="hwq_pool", bufs=LAG + 1))
-        stage_pool = ctx.enter_context(tc.tile_pool(name="stage_pool", bufs=3))
+        stage_pool = ctx.enter_context(tc.tile_pool(name="stage_pool", bufs=6))
         t_psum = ctx.enter_context(tc.psum_pool(name="t_psum", bufs=4))
         h_psum = ctx.enter_context(tc.psum_pool(name="h_psum", bufs=2))
         o_psum = ctx.enter_context(tc.psum_pool(name="o_psum", bufs=2))
@@ -73,12 +73,15 @@ def tile_linearmoloralayer_pa_t_kernel(tc, x, gate_logits, W_base, b_base, A, B,
         nc.sync.dma_start(out=gate_sb[:], in_=gate_view)
         for c in range(PACK):
             nc.sync.dma_start(out=a_raw[c][:], in_=a_view[:, c, :])
-        load_x(0, 2 * ROUND)
+        load_x(0, LAG * UNIT)
         nc.sync.dma_start(out=w_raw[:].rearrange("m (h d) -> m h d", h=O_TILES), in_=w_view)
-        load_x(2 * ROUND, 3 * ROUND)
-        nc.sync.dma_start(out=b_raw[:].rearrange("m (e f) -> m e f", e=E), in_=b_view)
+        load_x(LAG * UNIT, (LAG + 2) * UNIT)
+        for h in range(O_TILES):
+            nc.sync.dma_start(
+                out=b_raw[:, h * ER : (h + 1) * ER].rearrange("m (e r) -> m e r", r=RANK), in_=b_view[h]
+            )
         nc.sync.dma_start(out=bias_sb[:], in_=b_base.partition_broadcast(P))
-        load_x(3 * ROUND, SLOTS)
+        load_x((LAG + 2) * UNIT, SLOTS)
 
         def transpose_rows(bank, words):
             for block in range(WORDS // P):
@@ -118,25 +121,25 @@ def tile_linearmoloralayer_pa_t_kernel(tc, x, gate_logits, W_base, b_base, A, B,
             )
             nc.vector.reciprocal(out=g_inv[:, first:last], in_=g_sum[:, first:last])
 
-        def expand_route(r):
-            first = r * ROUND
-            wide = route_pool.tile([P, ROUND * P], F32, name="route_wide", tag="route_wide")
-            route_wide[r] = wide
-            shape = [P, ROUND, E, PACK]
+        def expand_route(n):
+            first = n * UNIT
+            wide = route_pool.tile([P, UNIT * P], F32, name="route_wide", tag="route_wide")
+            route_wide[n] = wide
+            shape = [P, UNIT, E, PACK]
             nc.gpsimd.tensor_tensor(
-                out=wide[:].rearrange("p (s e i) -> p s e i", s=ROUND, i=PACK),
-                in0=by_slot(g_exp[:, first * E : (first + ROUND) * E]).unsqueeze(3).to_broadcast(shape),
-                in1=g_inv[:, first : first + ROUND].unsqueeze(2).unsqueeze(3).to_broadcast(shape),
+                out=wide[:].rearrange("p (j e i) -> p j e i", j=UNIT, i=PACK),
+                in0=by_slot(g_exp[:, first * E : (first + UNIT) * E]).unsqueeze(3).to_broadcast(shape),
+                in1=g_inv[:, first : first + UNIT].unsqueeze(2).unsqueeze(3).to_broadcast(shape),
                 op=ALU.mult,
             )
 
-        def transpose_route(r):
-            bank = t_psum.tile([P, BANK], F32, name="route_bank", tag="t")
-            for j in range(ROUND):
+        def transpose_route(n):
+            bank = t_psum.tile([P, UNIT * P], F32, name="route_bank", tag="t")
+            for j in range(UNIT):
                 cols = slice(j * P, (j + 1) * P)
-                nc.tensor.transpose(out=bank[:, cols], in_=route_wide[r][:, cols], identity=ident[:])
-            route_t[r] = route_pool.tile([P, ROUND * P], F32, name="route_t", tag="route_t")
-            nc.scalar.mul(out=route_t[r][:], in_=bank[:], mul=SCALING)
+                nc.tensor.transpose(out=bank[:, cols], in_=route_wide[n][:, cols], identity=ident[:])
+            route_t[n] = route_pool.tile([P, UNIT * P], F32, name="route_t", tag="route_t")
+            nc.scalar.mul(out=route_t[n][:], in_=bank[:], mul=SCALING)
 
         a_grouped = keep.tile([P, PACK * D], BF16, align_bytes=64)
         a_codes = keep.tile([P, PACK * PASSES * P], U32, align_bytes=64)
@@ -144,7 +147,6 @@ def tile_linearmoloralayer_pa_t_kernel(tc, x, gate_logits, W_base, b_base, A, B,
         w_grouped = keep.tile([P, O_TILES * D], BF16, align_bytes=64)
         w_codes = keep.tile([P, PASSES * O], U32, align_bytes=64)
         w_scales = keep.tile([P, PASSES * O], U8, align_bytes=64)
-        b_sorted = keep.tile([P, O_TILES * ER], BF16)
         b_grouped = keep.tile([P, O * PACK], BF16, align_bytes=64)
         b_codes = keep.tile([P, O], U32, align_bytes=64)
         b_scales = keep.tile([P, O], U8, align_bytes=64)
@@ -177,22 +179,16 @@ def tile_linearmoloralayer_pa_t_kernel(tc, x, gate_logits, W_base, b_base, A, B,
                 out=w_codes[:].bitcast(FP8X4), scales=w_scales[:], in_=w_grouped[:]
             )
 
-        def sort_b():
-            nc.gpsimd.tensor_copy(
-                out=b_sorted[:].rearrange("m (h e r) -> m h e r", h=O_TILES, r=RANK),
-                in_=b_raw[:].rearrange("m (e h r) -> m h e r", h=O_TILES, r=RANK),
-            )
-
         def transpose_b():
-            words = b_sorted[:].bitcast(F32).rearrange("m (h q u) -> m h u q", h=O_TILES, u=2)
+            words = b_raw[:].bitcast(F32).rearrange("m (h q u) -> m h u q", h=O_TILES, u=2)
             bank = t_psum.tile([P, BANK], F32, name="b_bank", tag="t")
             for h in range(O_TILES):
                 for u in range(2):
                     cols = slice((h * 2 + u) * P, (h * 2 + u + 1) * P)
                     nc.tensor.transpose(out=bank[:, cols], in_=words[:, h, u, :], identity=ident[:])
             nc.scalar.copy(
-                out=b_grouped[:].bitcast(F32).rearrange("q (m h u) -> q m h u", h=O_TILES, u=2),
-                in_=bank[:].rearrange("q (h u m) -> q m h u", h=O_TILES, u=2),
+                out=b_grouped[:].bitcast(F32).rearrange("q (h m u) -> q h m u", h=O_TILES, u=2),
+                in_=bank[:].rearrange("q (h u m) -> q h m u", h=O_TILES, u=2),
             )
 
         def quantise_b():
@@ -204,149 +200,144 @@ def tile_linearmoloralayer_pa_t_kernel(tc, x, gate_logits, W_base, b_base, A, B,
         x_codes = {}
         x_scales = {}
 
-        def transpose_x(r):
-            x_grouped[r] = xg_pool.tile([P, ROUND * D], BF16, name="x_grouped", tag="xg", align_bytes=64)
-            grouped_words = x_grouped[r][:].bitcast(F32).rearrange(
-                "q (j g w u) -> q j g w u", j=ROUND, g=PASSES, u=2
+        def transpose_x(n):
+            x_grouped[n] = xg_pool.tile([P, UNIT * D], BF16, name="x_grouped", tag="xg", align_bytes=64)
+            grouped_words = x_grouped[n][:].bitcast(F32).rearrange(
+                "q (j g w u) -> q j g w u", j=UNIT, g=PASSES, u=2
             )
-            for j in range(ROUND):
+            for j in range(UNIT):
                 bank = t_psum.tile([P, BANK], F32, name="x_bank", tag="t")
-                transpose_rows(bank, x_raw[r * ROUND + j][:].bitcast(F32))
+                transpose_rows(bank, x_raw[n * UNIT + j][:].bitcast(F32))
                 nc.scalar.copy(out=grouped_words[:, j], in_=words_side_by_side(bank))
 
-        def quantise_x(r, j):
-            if j == 0:
-                width = ROUND * PASSES * P
-                x_codes[r] = xq_pool.tile([P, width], U32, name="x_codes", tag="xc", align_bytes=64)
-                x_scales[r] = xq_pool.tile([P, width], U8, name="x_scales", tag="xs", align_bytes=64)
-            cols = slice(j * PASSES * P, (j + 1) * PASSES * P)
+        def quantise_x(n):
+            width = UNIT * PASSES * P
+            x_codes[n] = xq_pool.tile([P, width], U32, name="x_codes", tag="xc", align_bytes=64)
+            x_scales[n] = xq_pool.tile([P, width], U8, name="x_scales", tag="xs", align_bytes=64)
             nc.vector.quantize_mx(
-                out=x_codes[r][:, cols].bitcast(FP8X4),
-                scales=x_scales[r][:, cols],
-                in_=x_grouped[r][:, j * D : (j + 1) * D],
+                out=x_codes[n][:].bitcast(FP8X4), scales=x_scales[n][:], in_=x_grouped[n][:]
             )
 
         hw_grouped = {}
         hw_codes = {}
         hw_scales = {}
+        h_banks = {}
         o_banks = {}
-        o_stage = {}
 
-        def project(r, j):
-            h_bank = h_psum.tile([P, BANK], F32, name="h_bank", tag="h")
-            for c in range(PACK):
+        def project(n):
+            h_banks[n] = []
+            for j in range(UNIT):
+                h_bank = h_psum.tile([P, BANK], F32, name="h_bank", tag="h")
+                h_banks[n].append(h_bank)
+                for c in range(PACK):
+                    for g in range(PASSES):
+                        a_cols = slice((c * PASSES + g) * P, (c * PASSES + g + 1) * P)
+                        x_cols = slice((j * PASSES + g) * P, (j * PASSES + g + 1) * P)
+                        nc.tensor.matmul_mx(
+                            out=h_bank[:, c * P : (c + 1) * P],
+                            lhsT=a_codes[:, a_cols].bitcast(FP8X4),
+                            lhsT_scale=a_scales[:, a_cols],
+                            rhs=x_codes[n][:, x_cols].bitcast(FP8X4),
+                            rhs_scale=x_scales[n][:, x_cols],
+                            start=(g == 0),
+                            stop=(g == PASSES - 1),
+                        )
+
+        def gate_h(n):
+            hw_grouped[n] = hwg_pool.tile([P, UNIT * ER], BF16, name="hw_grouped", tag="hwg", align_bytes=64)
+            for j in range(UNIT):
+                nc.vector.tensor_tensor(
+                    out=hw_grouped[n][:, j * ER : (j + 1) * ER].rearrange("q (w c) -> q w c", c=PACK),
+                    in0=h_banks[n][j][:].rearrange("q (c w) -> q w c", c=PACK),
+                    in1=route_t[n][:, j * P : (j + 1) * P].unsqueeze(2).to_broadcast([P, P, PACK]),
+                    op=ALU.mult,
+                )
+
+        def quantise_hw(n):
+            hw_codes[n] = hwq_pool.tile([P, UNIT * P], U32, name="hw_codes", tag="hc", align_bytes=64)
+            hw_scales[n] = hwq_pool.tile([P, UNIT * P], U8, name="hw_scales", tag="hs", align_bytes=64)
+            nc.vector.quantize_mx(
+                out=hw_codes[n][:].bitcast(FP8X4), scales=hw_scales[n][:], in_=hw_grouped[n][:]
+            )
+
+        def emit_output(n):
+            o_banks[n] = o_psum.tile([P, BANK], F32, name="o_bank", tag="o")
+            for j in range(UNIT):
+                o_cols = slice(j * O, (j + 1) * O)
                 for g in range(PASSES):
-                    a_cols = slice((c * PASSES + g) * P, (c * PASSES + g + 1) * P)
                     x_cols = slice((j * PASSES + g) * P, (j * PASSES + g + 1) * P)
                     nc.tensor.matmul_mx(
-                        out=h_bank[:, c * P : (c + 1) * P],
-                        lhsT=a_codes[:, a_cols].bitcast(FP8X4),
-                        lhsT_scale=a_scales[:, a_cols],
-                        rhs=x_codes[r][:, x_cols].bitcast(FP8X4),
-                        rhs_scale=x_scales[r][:, x_cols],
+                        out=o_banks[n][:, o_cols],
+                        lhsT=x_codes[n][:, x_cols].bitcast(FP8X4),
+                        lhsT_scale=x_scales[n][:, x_cols],
+                        rhs=w_codes[:, g * O : (g + 1) * O].bitcast(FP8X4),
+                        rhs_scale=w_scales[:, g * O : (g + 1) * O],
                         start=(g == 0),
-                        stop=(g == PASSES - 1),
+                        stop=False,
                     )
-            if j == 0:
-                hw_grouped[r] = hwg_pool.tile(
-                    [P, ROUND * ER], BF16, name="hw_grouped", tag="hwg", align_bytes=64
-                )
-            nc.vector.tensor_tensor(
-                out=hw_grouped[r][:, j * ER : (j + 1) * ER].rearrange("q (w c) -> q w c", c=PACK),
-                in0=h_bank[:].rearrange("q (c w) -> q w c", c=PACK),
-                in1=route_t[r][:, j * P : (j + 1) * P].unsqueeze(2).to_broadcast([P, P, PACK]),
-                op=ALU.mult,
-            )
-
-        def quantise_hw(r):
-            hw_codes[r] = hwq_pool.tile([P, ROUND * P], U32, name="hw_codes", tag="hc", align_bytes=64)
-            hw_scales[r] = hwq_pool.tile([P, ROUND * P], U8, name="hw_scales", tag="hs", align_bytes=64)
-            nc.vector.quantize_mx(
-                out=hw_codes[r][:].bitcast(FP8X4), scales=hw_scales[r][:], in_=hw_grouped[r][:]
-            )
-
-        def emit_output(r, j):
-            half = j % 2
-            if half == 0:
-                o_banks[r] = o_psum.tile([P, BANK], F32, name="o_bank", tag="o")
-            o_cols = slice(half * O, (half + 1) * O)
-            for g in range(PASSES):
-                x_cols = slice((j * PASSES + g) * P, (j * PASSES + g + 1) * P)
                 nc.tensor.matmul_mx(
-                    out=o_banks[r][:, o_cols],
-                    lhsT=x_codes[r][:, x_cols].bitcast(FP8X4),
-                    lhsT_scale=x_scales[r][:, x_cols],
-                    rhs=w_codes[:, g * O : (g + 1) * O].bitcast(FP8X4),
-                    rhs_scale=w_scales[:, g * O : (g + 1) * O],
-                    start=(g == 0),
-                    stop=False,
-                )
-            nc.tensor.matmul_mx(
-                out=o_banks[r][:, o_cols],
-                lhsT=hw_codes[r][:, j * P : (j + 1) * P].bitcast(FP8X4),
-                lhsT_scale=hw_scales[r][:, j * P : (j + 1) * P],
-                rhs=b_codes[:].bitcast(FP8X4),
-                rhs_scale=b_scales[:],
-                start=False,
-                stop=True,
-            )
-            if j == 0:
-                o_stage[r] = stage_pool.tile([P, ROUND * O], F32, name="o_stage", tag="os")
-            if half == 1:
-                nc.vector.tensor_tensor(
-                    out=o_stage[r][:, (j - 1) * O : (j + 1) * O].rearrange("p (s o) -> p s o", o=O),
-                    in0=o_banks[r][:].rearrange("p (s o) -> p s o", o=O),
-                    in1=bias_sb[:].unsqueeze(1).to_broadcast([P, 2, O]),
-                    op=ALU.add,
+                    out=o_banks[n][:, o_cols],
+                    lhsT=hw_codes[n][:, j * P : (j + 1) * P].bitcast(FP8X4),
+                    lhsT_scale=hw_scales[n][:, j * P : (j + 1) * P],
+                    rhs=b_codes[:].bitcast(FP8X4),
+                    rhs_scale=b_scales[:],
+                    start=False,
+                    stop=True,
                 )
 
-        def store(r):
+        def add_bias_and_store(n):
+            o_stage = stage_pool.tile([P, UNIT * O], F32, name="o_stage", tag="os")
+            nc.vector.tensor_tensor(
+                out=o_stage[:].rearrange("p (j o) -> p j o", o=O),
+                in0=o_banks[n][:].rearrange("p (j o) -> p j o", o=O),
+                in1=bias_sb[:].unsqueeze(1).to_broadcast([P, UNIT, O]),
+                op=ALU.add,
+            )
             nc.sync.dma_start(
-                out=out_view[:, r * ROUND : (r + 1) * ROUND, :],
-                in_=o_stage[r][:].rearrange("p (s o) -> p s o", o=O),
+                out=out_view[:, n * UNIT : (n + 1) * UNIT, :],
+                in_=o_stage[:].rearrange("p (j o) -> p j o", o=O),
             )
 
         warm = keep.tile([P, 1], F32)
         nc.vector.memset(warm[:], 0.0)
         nc.scalar.activation(out=warm[:], in_=warm[:], func=ACT.Exp)
 
-        softmax_shift(0, ROUND)
-        softmax_exp_norm(0, ROUND)
-        softmax_shift(ROUND, SLOTS)
+        head = 2 * UNIT
+        softmax_shift(0, head)
+        softmax_exp_norm(0, head)
+        softmax_shift(head, SLOTS)
         expand_route(0)
+        expand_route(1)
         for c in range(PACK):
             prepare_a_chunk(c)
-        softmax_exp_norm(ROUND, SLOTS)
-        expand_route(1)
         transpose_route(0)
         transpose_x(0)
-        for j in range(ROUND):
-            quantise_x(0, j)
+        quantise_x(0)
+        softmax_exp_norm(head, SLOTS)
 
-        for r in range(ROUNDS + LAG):
-            for j in range(ROUND):
-                if j == ROUND // 2 and r + 1 < ROUNDS:
-                    transpose_route(r + 1)
-                    transpose_x(r + 1)
-                    if r + 2 < ROUNDS:
-                        expand_route(r + 2)
-                    if r + 2 == LAG:
-                        transpose_w()
-                        sort_b()
-                    if r + 1 == LAG:
-                        transpose_b()
-                if r < ROUNDS:
-                    project(r, j)
-                if r >= LAG:
-                    emit_output(r - LAG, j)
-                if j >= ROUND // 2 and r + 1 < ROUNDS:
-                    quantise_x(r + 1, 2 * (j - ROUND // 2))
-                    quantise_x(r + 1, 2 * (j - ROUND // 2) + 1)
-            if r < ROUNDS:
-                quantise_hw(r)
-            if r + 2 == LAG:
+        for n in range(UNITS + LAG):
+            if n + 1 < UNITS:
+                transpose_route(n + 1)
+                transpose_x(n + 1)
+            if n + 2 < UNITS:
+                expand_route(n + 2)
+            if n + 2 == LAG:
+                transpose_w()
+            if n + 1 == LAG:
+                transpose_b()
+            if n < UNITS:
+                project(n)
+            if n >= LAG:
+                emit_output(n - LAG)
+            if n < UNITS:
+                gate_h(n)
+            if n + 1 < UNITS:
+                quantise_x(n + 1)
+            if n >= LAG:
+                add_bias_and_store(n - LAG)
+            if n < UNITS:
+                quantise_hw(n)
+            if n + 2 == LAG:
                 quantise_w()
-            if r + 1 == LAG:
+            if n + 1 == LAG:
                 quantise_b()
-            if r >= LAG:
-                store(r - LAG)

@@ -41,7 +41,7 @@ def tile_linearmoloralayer_pa_t_kernel(tc, x, gate_logits, W_base, b_base, A, B,
     out_view = out.flatten_outer_dims().rearrange("(p s) o -> p s o", s=SLOTS)
     a_view = A.flatten_outer_dims().rearrange("(q c) d -> q c d", c=PACK)
     w_view = W_base.rearrange("(h m) d -> m h d", m=P)
-    b_view = B.rearrange("e (h m) r -> h m e r", m=P)
+    b_view = B.rearrange("e (m h) r -> m e (h r)", h=O_TILES)
 
     with ExitStack() as ctx:
         keep = ctx.enter_context(tc.tile_pool(name="keep", bufs=1))
@@ -75,13 +75,10 @@ def tile_linearmoloralayer_pa_t_kernel(tc, x, gate_logits, W_base, b_base, A, B,
             nc.sync.dma_start(out=a_raw[c][:], in_=a_view[:, c, :])
         load_x(0, LAG * UNIT)
         nc.sync.dma_start(out=w_raw[:].rearrange("m (h d) -> m h d", h=O_TILES), in_=w_view)
-        load_x(LAG * UNIT, (LAG + 2) * UNIT)
-        for h in range(O_TILES):
-            nc.sync.dma_start(
-                out=b_raw[:, h * ER : (h + 1) * ER].rearrange("m (e r) -> m e r", r=RANK), in_=b_view[h]
-            )
+        nc.sync.dma_start(out=b_raw[:].rearrange("m (e f) -> m e f", e=E), in_=b_view)
+        load_x(LAG * UNIT, 2 * LAG * UNIT)
         nc.sync.dma_start(out=bias_sb[:], in_=b_base.partition_broadcast(P))
-        load_x((LAG + 2) * UNIT, SLOTS)
+        load_x(2 * LAG * UNIT, SLOTS)
 
         def transpose_rows(bank, words):
             for block in range(WORDS // P):
@@ -147,6 +144,7 @@ def tile_linearmoloralayer_pa_t_kernel(tc, x, gate_logits, W_base, b_base, A, B,
         w_grouped = keep.tile([P, O_TILES * D], BF16, align_bytes=64)
         w_codes = keep.tile([P, PASSES * O], U32, align_bytes=64)
         w_scales = keep.tile([P, PASSES * O], U8, align_bytes=64)
+        b_sorted = keep.tile([P, O_TILES * ER], BF16)
         b_grouped = keep.tile([P, O * PACK], BF16, align_bytes=64)
         b_codes = keep.tile([P, O], U32, align_bytes=64)
         b_scales = keep.tile([P, O], U8, align_bytes=64)
@@ -179,16 +177,22 @@ def tile_linearmoloralayer_pa_t_kernel(tc, x, gate_logits, W_base, b_base, A, B,
                 out=w_codes[:].bitcast(FP8X4), scales=w_scales[:], in_=w_grouped[:]
             )
 
+        def sort_b():
+            nc.vector.tensor_copy(
+                out=b_sorted[:].rearrange("m (h e r) -> m h e r", h=O_TILES, r=RANK),
+                in_=b_raw[:].rearrange("m (e h r) -> m h e r", h=O_TILES, r=RANK),
+            )
+
         def transpose_b():
-            words = b_raw[:].bitcast(F32).rearrange("m (h q u) -> m h u q", h=O_TILES, u=2)
+            words = b_sorted[:].bitcast(F32).rearrange("m (h q u) -> m h u q", h=O_TILES, u=2)
             bank = t_psum.tile([P, BANK], F32, name="b_bank", tag="t")
             for h in range(O_TILES):
                 for u in range(2):
                     cols = slice((h * 2 + u) * P, (h * 2 + u + 1) * P)
                     nc.tensor.transpose(out=bank[:, cols], in_=words[:, h, u, :], identity=ident[:])
             nc.scalar.copy(
-                out=b_grouped[:].bitcast(F32).rearrange("q (h m u) -> q h m u", h=O_TILES, u=2),
-                in_=bank[:].rearrange("q (h u m) -> q h m u", h=O_TILES, u=2),
+                out=b_grouped[:].bitcast(F32).rearrange("q (m h u) -> q m h u", h=O_TILES, u=2),
+                in_=bank[:].rearrange("q (h u m) -> q m h u", h=O_TILES, u=2),
             )
 
         def quantise_b():
@@ -337,6 +341,8 @@ def tile_linearmoloralayer_pa_t_kernel(tc, x, gate_logits, W_base, b_base, A, B,
                 add_bias_and_store(n - LAG)
             if n < UNITS:
                 quantise_hw(n)
+            if n + 3 == LAG:
+                sort_b()
             if n + 2 == LAG:
                 quantise_w()
             if n + 1 == LAG:

from contextlib import ExitStack

import concourse.masks as masks
import concourse.mybir as mybir

F32 = mybir.dt.float32
BF16 = mybir.dt.bfloat16
U32 = mybir.dt.uint32
U8 = mybir.dt.uint8
FP8X4 = mybir.dt.float8_e4m3fn_x4
ALU = mybir.AluOpType
ACT = mybir.ActivationFunctionType
AXIS = mybir.AxisListType

P = 128
PACK = 4
TOKENS = 4096
D = 1024
O = 256
E = 32
RANK = 16
ER = E * RANK
SCALING = 2.0
PASSES = D // (P * PACK)
WORDS = D // 2
BANK = 512
SLOTS = TOKENS // P
UNIT = 2
UNITS = SLOTS // UNIT
O_TILES = O // P
LAG = 4

FLOPS = 2 * TOKENS * D * (O + ER) + 2 * TOKENS * ER * O


def tile_linearmoloralayer_pa_t_kernel(tc, x, gate_logits, W_base, b_base, A, B, out):
    nc = tc.nc

    x_view = x.flatten_outer_dims().rearrange("(p s) d -> p s d", s=SLOTS)
    gate_view = gate_logits.flatten_outer_dims().rearrange("(p s) e -> p (s e)", s=SLOTS)
    out_view = out.flatten_outer_dims().rearrange("(p s) o -> p s o", s=SLOTS)
    a_view = A.flatten_outer_dims().rearrange("(q c) d -> q c d", c=PACK)
    w_view = W_base.rearrange("(h m) d -> m h d", m=P)
    b_view = B.rearrange("e (m h) r -> m e (h r)", h=O_TILES)

    with ExitStack() as ctx:
        keep = ctx.enter_context(tc.tile_pool(name="keep", bufs=1))
        xg_pool = ctx.enter_context(tc.tile_pool(name="xg_pool", bufs=2))
        xq_pool = ctx.enter_context(tc.tile_pool(name="xq_pool", bufs=LAG + 2))
        route_pool = ctx.enter_context(tc.tile_pool(name="route_pool", bufs=2))
        hwg_pool = ctx.enter_context(tc.tile_pool(name="hwg_pool", bufs=2))
        hwq_pool = ctx.enter_context(tc.tile_pool(name="hwq_pool", bufs=LAG + 1))
        stage_pool = ctx.enter_context(tc.tile_pool(name="stage_pool", bufs=6))
        t_psum = ctx.enter_context(tc.psum_pool(name="t_psum", bufs=4))
        h_psum = ctx.enter_context(tc.psum_pool(name="h_psum", bufs=2))
        o_psum = ctx.enter_context(tc.psum_pool(name="o_psum", bufs=2))
        ctx.enter_context(tc.manual_schedule())

        ident = keep.tile([P, P], F32)
        masks.make_identity(nc, ident[:])

        gate_sb = keep.tile([P, SLOTS * E], BF16)
        a_raw = [keep.tile([P, D], BF16, name="a_raw%d" % c) for c in range(PACK)]
        x_raw = [keep.tile([P, D], BF16, name="x_raw%d" % s) for s in range(SLOTS)]
        w_raw = keep.tile([P, O_TILES * D], BF16)
        b_raw = keep.tile([P, O_TILES * ER], BF16)
        bias_sb = keep.tile([P, O], BF16)

        def load_x(first, last):
            for s in range(first, last):
                nc.sync.dma_start(out=x_raw[s][:], in_=x_view[:, s, :])

        nc.sync.dma_start(out=gate_sb[:], in_=gate_view)
        for c in range(PACK):
            nc.sync.dma_start(out=a_raw[c][:], in_=a_view[:, c, :])
        load_x(0, LAG * UNIT)
        nc.sync.dma_start(out=w_raw[:].rearrange("m (h d) -> m h d", h=O_TILES), in_=w_view)
        nc.sync.dma_start(out=b_raw[:].rearrange("m (e f) -> m e f", e=E), in_=b_view)
        load_x(LAG * UNIT, 2 * LAG * UNIT)
        nc.sync.dma_start(out=bias_sb[:], in_=b_base.partition_broadcast(P))
        load_x(2 * LAG * UNIT, SLOTS)

        def transpose_rows(bank, words):
            for block in range(WORDS // P):
                cols = slice(block * P, (block + 1) * P)
                nc.tensor.transpose(out=bank[:, cols], in_=words[:, cols], identity=ident[:])

        def words_side_by_side(bank):
            return bank[:].rearrange("q (g u m) -> q g m u", g=PASSES, u=2)

        g_max = keep.tile([P, SLOTS], F32)
        g_exp = keep.tile([P, SLOTS * E], F32)
        g_sum = keep.tile([P, SLOTS], F32)
        g_inv = keep.tile([P, SLOTS], F32)
        route_wide = {}
        route_t = {}

        def by_slot(ap):
            return ap.rearrange("p (s e) -> p s e", e=E)

        def softmax_shift(first, last):
            cols = slice(first * E, last * E)
            nc.vector.tensor_reduce(
                out=g_max[:, first:last], in_=by_slot(gate_sb[:, cols]), axis=AXIS.X, op=ALU.max
            )
            nc.vector.tensor_tensor(
                out=by_slot(g_exp[:, cols]),
                in0=by_slot(gate_sb[:, cols]),
                in1=g_max[:, first:last].unsqueeze(2).to_broadcast([P, last - first, E]),
                op=ALU.subtract,
            )

        def softmax_exp_norm(first, last):
            cols = slice(first * E, last * E)
            nc.scalar.activation(out=g_exp[:, cols], in_=g_exp[:, cols], func=ACT.Exp)
            nc.vector.tensor_reduce(
                out=g_sum[:, first:last], in_=by_slot(g_exp[:, cols]), axis=AXIS.X, op=ALU.add
            )
            nc.vector.reciprocal(out=g_inv[:, first:last], in_=g_sum[:, first:last])

        def expand_route(n):
            first = n * UNIT
            wide = route_pool.tile([P, UNIT * P], F32, name="route_wide", tag="route_wide")
            route_wide[n] = wide
            shape = [P, UNIT, E, PACK]
            nc.gpsimd.tensor_tensor(
                out=wide[:].rearrange("p (j e i) -> p j e i", j=UNIT, i=PACK),
                in0=by_slot(g_exp[:, first * E : (first + UNIT) * E]).unsqueeze(3).to_broadcast(shape),
                in1=g_inv[:, first : first + UNIT].unsqueeze(2).unsqueeze(3).to_broadcast(shape),
                op=ALU.mult,
            )

        def transpose_route(n):
            bank = t_psum.tile([P, UNIT * P], F32, name="route_bank", tag="t")
            for j in range(UNIT):
                cols = slice(j * P, (j + 1) * P)
                nc.tensor.transpose(out=bank[:, cols], in_=route_wide[n][:, cols], identity=ident[:])
            route_t[n] = route_pool.tile([P, UNIT * P], F32, name="route_t", tag="route_t")
            nc.scalar.mul(out=route_t[n][:], in_=bank[:], mul=SCALING)

        a_grouped = keep.tile([P, PACK * D], BF16, align_bytes=64)
        a_codes = keep.tile([P, PACK * PASSES * P], U32, align_bytes=64)
        a_scales = keep.tile([P, PACK * PASSES * P], U8, align_bytes=64)
        w_grouped = keep.tile([P, O_TILES * D], BF16, align_bytes=64)
        w_codes = keep.tile([P, PASSES * O], U32, align_bytes=64)
        w_scales = keep.tile([P, PASSES * O], U8, align_bytes=64)
        b_sorted = keep.tile([P, O_TILES * ER], BF16)
        b_grouped = keep.tile([P, O * PACK], BF16, align_bytes=64)
        b_codes = keep.tile([P, O], U32, align_bytes=64)
        b_scales = keep.tile([P, O], U8, align_bytes=64)

        def prepare_a_chunk(c):
            bank = t_psum.tile([P, BANK], F32, name="a_bank", tag="t")
            transpose_rows(bank, a_raw[c][:].bitcast(F32))
            grouped_words = a_grouped[:].bitcast(F32).rearrange(
                "q (c g m u) -> q c g m u", c=PACK, g=PASSES, u=2
            )
            nc.scalar.copy(out=grouped_words[:, c], in_=words_side_by_side(bank))
            cols = slice(c * PASSES * P, (c + 1) * PASSES * P)
            nc.vector.quantize_mx(
                out=a_codes[:, cols].bitcast(FP8X4),
                scales=a_scales[:, cols],
                in_=a_grouped[:, c * D : (c + 1) * D],
            )

        def transpose_w():
            grouped_words = w_grouped[:].bitcast(F32).rearrange(
                "q (g h m u) -> q g h m u", g=PASSES, h=O_TILES, u=2
            )
            for h in range(O_TILES):
                bank = t_psum.tile([P, BANK], F32, name="w_bank", tag="t")
                transpose_rows(bank, w_raw[:].bitcast(F32)[:, h * WORDS : (h + 1) * WORDS])
                nc.scalar.copy(out=grouped_words[:, :, h], in_=words_side_by_side(bank))

        def quantise_w():
            nc.vector.quantize_mx(
                out=w_codes[:].bitcast(FP8X4), scales=w_scales[:], in_=w_grouped[:]
            )

        def sort_b():
            nc.vector.tensor_copy(
                out=b_sorted[:].rearrange("m (h e r) -> m h e r", h=O_TILES, r=RANK),
                in_=b_raw[:].rearrange("m (e h r) -> m h e r", h=O_TILES, r=RANK),
            )

        def transpose_b():
            words = b_sorted[:].bitcast(F32).rearrange("m (h q u) -> m h u q", h=O_TILES, u=2)
            bank = t_psum.tile([P, BANK], F32, name="b_bank", tag="t")
            for h in range(O_TILES):
                for u in range(2):
                    cols = slice((h * 2 + u) * P, (h * 2 + u + 1) * P)
                    nc.tensor.transpose(out=bank[:, cols], in_=words[:, h, u, :], identity=ident[:])
            nc.scalar.copy(
                out=b_grouped[:].bitcast(F32).rearrange("q (m h u) -> q m h u", h=O_TILES, u=2),
                in_=bank[:].rearrange("q (h u m) -> q m h u", h=O_TILES, u=2),
            )

        def quantise_b():
            nc.vector.quantize_mx(
                out=b_codes[:].bitcast(FP8X4), scales=b_scales[:], in_=b_grouped[:]
            )

        x_grouped = {}
        x_codes = {}
        x_scales = {}

        def transpose_x(n):
            x_grouped[n] = xg_pool.tile([P, UNIT * D], BF16, name="x_grouped", tag="xg", align_bytes=64)
            grouped_words = x_grouped[n][:].bitcast(F32).rearrange(
                "q (j g w u) -> q j g w u", j=UNIT, g=PASSES, u=2
            )
            for j in range(UNIT):
                bank = t_psum.tile([P, BANK], F32, name="x_bank", tag="t")
                transpose_rows(bank, x_raw[n * UNIT + j][:].bitcast(F32))
                nc.scalar.copy(out=grouped_words[:, j], in_=words_side_by_side(bank))

        def quantise_x(n):
            width = UNIT * PASSES * P
            x_codes[n] = xq_pool.tile([P, width], U32, name="x_codes", tag="xc", align_bytes=64)
            x_scales[n] = xq_pool.tile([P, width], U8, name="x_scales", tag="xs", align_bytes=64)
            nc.vector.quantize_mx(
                out=x_codes[n][:].bitcast(FP8X4), scales=x_scales[n][:], in_=x_grouped[n][:]
            )

        hw_grouped = {}
        hw_codes = {}
        hw_scales = {}
        h_banks = {}
        o_banks = {}

        def project(n):
            h_banks[n] = []
            for j in range(UNIT):
                h_bank = h_psum.tile([P, BANK], F32, name="h_bank", tag="h")
                h_banks[n].append(h_bank)
                for c in range(PACK):
                    for g in range(PASSES):
                        a_cols = slice((c * PASSES + g) * P, (c * PASSES + g + 1) * P)
                        x_cols = slice((j * PASSES + g) * P, (j * PASSES + g + 1) * P)
                        nc.tensor.matmul_mx(
                            out=h_bank[:, c * P : (c + 1) * P],
                            lhsT=a_codes[:, a_cols].bitcast(FP8X4),
                            lhsT_scale=a_scales[:, a_cols],
                            rhs=x_codes[n][:, x_cols].bitcast(FP8X4),
                            rhs_scale=x_scales[n][:, x_cols],
                            start=(g == 0),
                            stop=(g == PASSES - 1),
                        )

        def gate_h(n):
            hw_grouped[n] = hwg_pool.tile([P, UNIT * ER], BF16, name="hw_grouped", tag="hwg", align_bytes=64)
            for j in range(UNIT):
                nc.vector.tensor_tensor(
                    out=hw_grouped[n][:, j * ER : (j + 1) * ER].rearrange("q (w c) -> q w c", c=PACK),
                    in0=h_banks[n][j][:].rearrange("q (c w) -> q w c", c=PACK),
                    in1=route_t[n][:, j * P : (j + 1) * P].unsqueeze(2).to_broadcast([P, P, PACK]),
                    op=ALU.mult,
                )

        def quantise_hw(n):
            hw_codes[n] = hwq_pool.tile([P, UNIT * P], U32, name="hw_codes", tag="hc", align_bytes=64)
            hw_scales[n] = hwq_pool.tile([P, UNIT * P], U8, name="hw_scales", tag="hs", align_bytes=64)
            nc.vector.quantize_mx(
                out=hw_codes[n][:].bitcast(FP8X4), scales=hw_scales[n][:], in_=hw_grouped[n][:]
            )

        def emit_output(n):
            o_banks[n] = o_psum.tile([P, BANK], F32, name="o_bank", tag="o")
            for j in range(UNIT):
                o_cols = slice(j * O, (j + 1) * O)
                for g in range(PASSES):
                    x_cols = slice((j * PASSES + g) * P, (j * PASSES + g + 1) * P)
                    nc.tensor.matmul_mx(
                        out=o_banks[n][:, o_cols],
                        lhsT=x_codes[n][:, x_cols].bitcast(FP8X4),
                        lhsT_scale=x_scales[n][:, x_cols],
                        rhs=w_codes[:, g * O : (g + 1) * O].bitcast(FP8X4),
                        rhs_scale=w_scales[:, g * O : (g + 1) * O],
                        start=(g == 0),
                        stop=False,
                    )
                nc.tensor.matmul_mx(
                    out=o_banks[n][:, o_cols],
                    lhsT=hw_codes[n][:, j * P : (j + 1) * P].bitcast(FP8X4),
                    lhsT_scale=hw_scales[n][:, j * P : (j + 1) * P],
                    rhs=b_codes[:].bitcast(FP8X4),
                    rhs_scale=b_scales[:],
                    start=False,
                    stop=True,
                )

        def add_bias_and_store(n):
            o_stage = stage_pool.tile([P, UNIT * O], F32, name="o_stage", tag="os")
            nc.vector.tensor_tensor(
                out=o_stage[:].rearrange("p (j o) -> p j o", o=O),
                in0=o_banks[n][:].rearrange("p (j o) -> p j o", o=O),
                in1=bias_sb[:].unsqueeze(1).to_broadcast([P, UNIT, O]),
                op=ALU.add,
            )
            nc.sync.dma_start(
                out=out_view[:, n * UNIT : (n + 1) * UNIT, :],
                in_=o_stage[:].rearrange("p (j o) -> p j o", o=O),
            )

        warm = keep.tile([P, 1], F32)
        nc.vector.memset(warm[:], 0.0)
        nc.scalar.activation(out=warm[:], in_=warm[:], func=ACT.Exp)

        head = 2 * UNIT
        softmax_shift(0, head)
        softmax_exp_norm(0, head)
        softmax_shift(head, SLOTS)
        expand_route(0)
        expand_route(1)
        for c in range(PACK):
            prepare_a_chunk(c)
        transpose_route(0)
        transpose_x(0)
        quantise_x(0)
        softmax_exp_norm(head, SLOTS)

        for n in range(UNITS + LAG):
            if n + 1 < UNITS:
                transpose_route(n + 1)
                transpose_x(n + 1)
            if n + 2 < UNITS:
                expand_route(n + 2)
            if n + 2 == LAG:
                transpose_w()
            if n + 1 == LAG:
                transpose_b()
            if n < UNITS:
                project(n)
            if n >= LAG:
                emit_output(n - LAG)
            if n < UNITS:
                gate_h(n)
            if n + 1 < UNITS:
                quantise_x(n + 1)
            if n >= LAG:
                add_bias_and_store(n - LAG)
            if n < UNITS:
                quantise_hw(n)
            if n + 3 == LAG:
                sort_b()
            if n + 2 == LAG:
                quantise_w()
            if n + 1 == LAG:
                quantise_b()
